import numpy as np
import ml_dtypes


def mxq(x, axis, fmt="e4m3"):
    dtype, down = {"e4m3": (ml_dtypes.float8_e4m3fn, 7), "e5m2": (ml_dtypes.float8_e5m2, 14)}[fmt]
    v = np.moveaxis(np.asarray(x, np.float32).astype(ml_dtypes.bfloat16).astype(np.float64), axis, -1)
    blocks = v.reshape(v.shape[:-1] + (-1, 32))
    amax = np.abs(blocks).max(-1, keepdims=True)
    byte = np.maximum(np.where(amax > 0, np.frexp(amax)[1] - 1 + 127, 0) - down, 1)
    scale = np.exp2(byte - 127.0)
    codes = (blocks / scale).astype(np.float32).astype(dtype).astype(np.float64)
    return np.moveaxis((codes * scale).reshape(v.shape), -1, axis)


WIDE = False


def mx_kscale(k):
    if not WIDE:
        return np.ones(k)
    levels = np.array([20, -20, 10, -10, 0])
    a = np.random.permutation(np.resize(levels, k // 512 * 4)).reshape(k // 512, 4)
    idx = np.arange(k)
    return np.exp2(a[idx // 512, idx % 128 // 32])


BF16 = ml_dtypes.bfloat16


def bf(x):
    return np.asarray(x, np.float32).astype(BF16)


def f64(x):
    return np.asarray(x).astype(np.float64)


N, Ci, H, W, Co = 2, 128, 16, 16, 16384
TAPS = [(1, 1), (0, 1), (1, 0), (1, 2), (2, 1)]
K = len(TAPS)
PAD = 1


def setup_inputs():
    u = mx_kscale(Co)
    x = np.random.standard_normal((N, Ci, H, W))
    weight = np.random.standard_normal((Co, Ci, K)) / np.sqrt(Ci * K) / u[:, None, None]
    g = np.random.standard_normal((N, Co, H, W)) * np.exp2(np.random.randint(-12, 1, (N, 1, H, W))) * 16.0 * u[None, :, None, None]
    return {"x": bf(x), "weight": bf(weight), "grad_out": bf(g)}


def reference(x, weight, grad_out):
    gq = mxq(f64(grad_out), 1, "e5m2").transpose(1, 0, 2, 3).reshape(Co, N * H * W)
    wq = mxq(f64(weight), 0, "e4m3")
    gx = np.zeros((N, Ci, H, W))
    for k, (dy, dx) in enumerate(TAPS):
        z = (wq[:, :, k].T @ gq).reshape(Ci, N, H, W).transpose(1, 0, 2, 3)
        zp = np.pad(z, ((0, 0), (0, 0), (PAD, PAD), (PAD, PAD)))
        ry, rx = 2 * PAD - dy, 2 * PAD - dx
        gx = gx + zp[:, :, ry:ry + H, rx:rx + W]
    return gx

@@ -1,0 +1,124 @@
+from contextlib import ExitStack
+
+import concourse.mybir as mybir
+
+BF16 = mybir.dt.bfloat16
+F32 = mybir.dt.float32
+U32 = mybir.dt.uint32
+U8 = mybir.dt.uint8
+E4M3X4 = mybir.dt.float8_e4m3fn_x4
+E5M2X4 = mybir.dt.float8_e5m2_x4
+
+P = 128
+PACK = 4
+K_PASS = P * PACK
+
+IMAGES, CI, H, W, CO = 2, 128, 16, 16, 16384
+PIXELS = H * W
+COLUMNS = IMAGES * PIXELS
+EY = (0, -1, 0, 0, 1)
+EX = (0, 0, -1, 1, 0)
+TAPS = len(EY)
+PASSES = CO // K_PASS
+
+FLOPS = 2 * CO * CI * TAPS * COLUMNS
+BYTES = 2 * CO * CI * TAPS + 2 * IMAGES * CO * PIXELS + 4 * IMAGES * CI * PIXELS
+
+TAPS_FIRST = 4
+
+RAW_BUFS = 6
+WORK_BUFS = 3
+
+
+def tile_spatialconv_pa_k_kernel(tc, x, weight, grad_out, out):
+    nc = tc.nc
+    w_rows = weight.rearrange("(g p j) c t -> g p (j c t)", p=P, j=PACK)
+    g_rows = grad_out.rearrange("n (g p j) h w -> g p n (j h w)", p=P, j=PACK)
+
+    with ExitStack() as ctx:
+        raw = ctx.enter_context(tc.tile_pool(name="raw", bufs=RAW_BUFS))
+        work = ctx.enter_context(tc.tile_pool(name="work", bufs=WORK_BUFS))
+        last = ctx.enter_context(tc.tile_pool(name="last", bufs=1))
+        psum = ctx.enter_context(tc.psum_pool(name="psum", bufs=1))
+        ctx.enter_context(tc.manual_schedule())
+
+        z = [psum.tile([P, IMAGES, H, W], F32, name="z%d" % t) for t in range(TAPS)]
+
+        grouped = {}
+        quantised = {}
+
+        def load_and_regroup(g):
+            w_raw = raw.tile([P, PACK, CI, TAPS], BF16)
+            nc.sync.dma_start(out=w_raw[:].rearrange("p j c t -> p (j c t)"), in_=w_rows[g])
+            g_raw = raw.tile([P, IMAGES, PACK, PIXELS], BF16)
+            nc.sync.dma_start(out=g_raw[:].rearrange("p n j x -> p n (j x)"), in_=g_rows[g])
+
+            w_grouped = work.tile([P, TAPS, CI, PACK], BF16, align_bytes=64)
+            nc.vector.tensor_copy(
+                out=w_grouped[:].rearrange("p t (s c) j -> p s t c j", s=2),
+                in_=w_raw[:].rearrange("p j (s c) t -> p s t c j", s=2),
+            )
+            g_grouped = work.tile([P, IMAGES, PIXELS, PACK], BF16, align_bytes=64)
+            for n in range(IMAGES):
+                nc.scalar.copy(
+                    out=g_grouped[:, n].rearrange("p (b i) j -> p b j i", i=4),
+                    in_=g_raw[:, n].rearrange("p j (b i) -> p b j i", i=4),
+                )
+            grouped[g] = (w_grouped, g_grouped)
+
+        def quantise(g):
+            w_grouped, g_grouped = grouped.pop(g)
+            g_codes = work.tile([P, COLUMNS], U32, align_bytes=64)
+            g_scales = work.tile([P, COLUMNS], U8, align_bytes=64)
+            nc.vector.quantize_mx(
+                out=g_codes[:].bitcast(E5M2X4),
+                scales=g_scales[:],
+                in_=g_grouped[:].rearrange("p n x j -> p (n x j)"),
+            )
+            w_codes = work.tile([P, TAPS * CI], U32, align_bytes=64)
+            w_scales = work.tile([P, TAPS * CI], U8, align_bytes=64)
+            w_flat = w_grouped[:].rearrange("p t c j -> p (t c j)")
+            for lo, hi in ((0, TAPS_FIRST * CI), (TAPS_FIRST * CI, TAPS * CI)):
+                nc.vector.quantize_mx(
+                    out=w_codes[:, lo:hi].bitcast(E4M3X4),
+                    scales=w_scales[:, lo:hi],
+                    in_=w_flat[:, PACK * lo : PACK * hi],
+                )
+            quantised[g] = (w_codes, w_scales, g_codes, g_scales)
+
+        def multiply(g):
+            w_codes, w_scales, g_codes, g_scales = quantised.pop(g)
+            for t in range(TAPS):
+                nc.tensor.matmul_mx(
+                    out=z[t][:].rearrange("p n h w -> p (n h w)"),
+                    lhsT=w_codes[:, t * CI : (t + 1) * CI].bitcast(E4M3X4),
+                    lhsT_scale=w_scales[:, t * CI : (t + 1) * CI],
+                    rhs=g_codes[:].bitcast(E5M2X4),
+                    rhs_scale=g_scales[:],
+                    start=(g == 0),
+                    stop=(g == PASSES - 1),
+                )
+
+        load_and_regroup(0)
+        for g in range(1, PASSES):
+            load_and_regroup(g)
+            quantise(g - 1)
+            multiply(g - 1)
+        quantise(PASSES - 1)
+        multiply(PASSES - 1)
+
+        total = last.tile([P, IMAGES, H, W], F32)
+        nc.scalar.copy(out=total[:], in_=z[0][:])
+        for t in range(1, TAPS):
+            h_lo, h_hi = max(0, EY[t]), H + min(0, EY[t])
+            w_lo, w_hi = max(0, EX[t]), W + min(0, EX[t])
+            nc.vector.tensor_tensor(
+                out=total[:, :, h_lo:h_hi, w_lo:w_hi],
+                in0=total[:, :, h_lo:h_hi, w_lo:w_hi],
+                in1=z[t][:, :, h_lo - EY[t] : h_hi - EY[t], w_lo - EX[t] : w_hi - EX[t]],
+                op=mybir.AluOpType.add,
+            )
+        nc.sync.dma_start(
+            out=out.rearrange("n c h w -> c n (h w)"),
+            in_=total[:].rearrange("p n h w -> p n (h w)"),
+        )

@@ -26,6 +26,8 @@ BYTES = 2 * CO * CI * TAPS + 2 * IMAGES * CO * PIXELS + 4 * IMAGES * CI * PIXELS
 
 TAPS_FIRST = 4
 
+TAP_RUNS = ((0, 3), (3, 5))
+
 RAW_BUFS = 6
 WORK_BUFS = 3
 
@@ -54,10 +56,11 @@ def tile_spatialconv_pa_k_kernel(tc, x, weight, grad_out, out):
             nc.sync.dma_start(out=g_raw[:].rearrange("p n j x -> p n (j x)"), in_=g_rows[g])
 
             w_grouped = work.tile([P, TAPS, CI, PACK], BF16, align_bytes=64)
-            nc.vector.tensor_copy(
-                out=w_grouped[:].rearrange("p t (s c) j -> p s t c j", s=2),
-                in_=w_raw[:].rearrange("p j (s c) t -> p s t c j", s=2),
-            )
+            for lo, hi in TAP_RUNS:
+                nc.vector.tensor_copy(
+                    out=w_grouped[:, lo:hi].rearrange("p t c j -> p c j t"),
+                    in_=w_raw[:, :, :, lo:hi].rearrange("p j c t -> p c j t"),
+                )
             g_grouped = work.tile([P, IMAGES, PIXELS, PACK], BF16, align_bytes=64)
             for n in range(IMAGES):
                 nc.scalar.copy(

@@ -58,8 +58,8 @@ def tile_spatialconv_pa_k_kernel(tc, x, weight, grad_out, out):
             w_grouped = work.tile([P, TAPS, CI, PACK], BF16, align_bytes=64)
             for lo, hi in TAP_RUNS:
                 nc.vector.tensor_copy(
-                    out=w_grouped[:, lo:hi].rearrange("p t c j -> p c j t"),
-                    in_=w_raw[:, :, :, lo:hi].rearrange("p j c t -> p c j t"),
+                    out=w_grouped[:, lo:hi].rearrange("p t (b i) j -> p b j t i", i=2),
+                    in_=w_raw[:, :, :, lo:hi].rearrange("p j (b i) t -> p b j t i", i=2),
                 )
             g_grouped = work.tile([P, IMAGES, PIXELS, PACK], BF16, align_bytes=64)
             for n in range(IMAGES):

@@ -26,7 +26,9 @@ BYTES = 2 * CO * CI * TAPS + 2 * IMAGES * CO * PIXELS + 4 * IMAGES * CI * PIXELS
 
 TAPS_FIRST = 4
 
-TAP_RUNS = ((0, 3), (3, 5))
+TAPS_A = slice(0, 3)
+TAPS_B = slice(3, 5)
+SCALAR_CHANNELS = 40
 
 RAW_BUFS = 6
 WORK_BUFS = 3
@@ -56,17 +58,22 @@ def tile_spatialconv_pa_k_kernel(tc, x, weight, grad_out, out):
             nc.sync.dma_start(out=g_raw[:].rearrange("p n j x -> p n (j x)"), in_=g_rows[g])
 
             w_grouped = work.tile([P, TAPS, CI, PACK], BF16, align_bytes=64)
-            for lo, hi in TAP_RUNS:
-                nc.vector.tensor_copy(
-                    out=w_grouped[:, lo:hi].rearrange("p t (b i) j -> p b j t i", i=2),
-                    in_=w_raw[:, :, :, lo:hi].rearrange("p j (b i) t -> p b j t i", i=2),
+
+            def regroup_weight(copy, taps, channels):
+                copy(
+                    out=w_grouped[:, taps, channels].rearrange("p t (b i) j -> p b j t i", i=2),
+                    in_=w_raw[:, :, channels, taps].rearrange("p j (b i) t -> p b j t i", i=2),
                 )
+
+            regroup_weight(nc.vector.tensor_copy, TAPS_A, slice(0, CI))
+            regroup_weight(nc.vector.tensor_copy, TAPS_B, slice(0, CI - SCALAR_CHANNELS))
             g_grouped = work.tile([P, IMAGES, PIXELS, PACK], BF16, align_bytes=64)
             for n in range(IMAGES):
                 nc.scalar.copy(
                     out=g_grouped[:, n].rearrange("p (b i) j -> p b j i", i=4),
                     in_=g_raw[:, n].rearrange("p j (b i) -> p b j i", i=4),
                 )
+            regroup_weight(nc.scalar.copy, TAPS_B, slice(CI - SCALAR_CHANNELS, CI))
             grouped[g] = (w_grouped, g_grouped)
 
         def quantise(g):

@@ -28,7 +28,7 @@ TAPS_FIRST = 4
 
 TAPS_A = slice(0, 3)
 TAPS_B = slice(3, 5)
-SCALAR_CHANNELS = 40
+VECTOR_PIXELS = 96
 
 RAW_BUFS = 6
 WORK_BUFS = 3
@@ -52,10 +52,10 @@ def tile_spatialconv_pa_k_kernel(tc, x, weight, grad_out, out):
         quantised = {}
 
         def load_and_regroup(g):
-            w_raw = raw.tile([P, PACK, CI, TAPS], BF16)
-            nc.sync.dma_start(out=w_raw[:].rearrange("p j c t -> p (j c t)"), in_=w_rows[g])
             g_raw = raw.tile([P, IMAGES, PACK, PIXELS], BF16)
             nc.sync.dma_start(out=g_raw[:].rearrange("p n j x -> p n (j x)"), in_=g_rows[g])
+            w_raw = raw.tile([P, PACK, CI, TAPS], BF16)
+            nc.sync.dma_start(out=w_raw[:].rearrange("p j c t -> p (j c t)"), in_=w_rows[g])
 
             w_grouped = work.tile([P, TAPS, CI, PACK], BF16, align_bytes=64)
 
@@ -65,15 +65,18 @@ def tile_spatialconv_pa_k_kernel(tc, x, weight, grad_out, out):
                     in_=w_raw[:, :, channels, taps].rearrange("p j (b i) t -> p b j t i", i=2),
                 )
 
-            regroup_weight(nc.vector.tensor_copy, TAPS_A, slice(0, CI))
-            regroup_weight(nc.vector.tensor_copy, TAPS_B, slice(0, CI - SCALAR_CHANNELS))
             g_grouped = work.tile([P, IMAGES, PIXELS, PACK], BF16, align_bytes=64)
-            for n in range(IMAGES):
-                nc.scalar.copy(
-                    out=g_grouped[:, n].rearrange("p (b i) j -> p b j i", i=4),
-                    in_=g_raw[:, n].rearrange("p j (b i) -> p b j i", i=4),
+
+            def regroup_grad(copy, pixels):
+                copy(
+                    out=g_grouped[:, :, pixels].rearrange("p n (b i) j -> p n b j i", i=4),
+                    in_=g_raw[:, :, :, pixels].rearrange("p n j (b i) -> p n b j i", i=4),
                 )
-            regroup_weight(nc.scalar.copy, TAPS_B, slice(CI - SCALAR_CHANNELS, CI))
+
+            regroup_grad(nc.vector.tensor_copy, slice(PIXELS - VECTOR_PIXELS, PIXELS))
+            regroup_grad(nc.scalar.copy, slice(0, PIXELS - VECTOR_PIXELS))
+            regroup_weight(nc.vector.tensor_copy, TAPS_A, slice(0, CI))
+            regroup_weight(nc.scalar.copy, TAPS_B, slice(0, CI))
             grouped[g] = (w_grouped, g_grouped)
 
         def quantise(g):
@@ -109,13 +112,10 @@ def tile_spatialconv_pa_k_kernel(tc, x, weight, grad_out, out):
                     stop=(g == PASSES - 1),
                 )
 
-        load_and_regroup(0)
-        for g in range(1, PASSES):
+        for g in range(PASSES):
             load_and_regroup(g)
-            quantise(g - 1)
-            multiply(g - 1)
-        quantise(PASSES - 1)
-        multiply(PASSES - 1)
+            quantise(g)
+            multiply(g)
 
         total = last.tile([P, IMAGES, H, W], F32)
         nc.scalar.copy(out=total[:], in_=z[0][:])

@@ -118,17 +118,20 @@ def tile_spatialconv_pa_k_kernel(tc, x, weight, grad_out, out):
             multiply(g)
 
         total = last.tile([P, IMAGES, H, W], F32)
-        nc.scalar.copy(out=total[:], in_=z[0][:])
+        for n in range(IMAGES):
+            nc.scalar.copy(out=total[:, n], in_=z[0][:, n])
         for t in range(1, TAPS):
             h_lo, h_hi = max(0, EY[t]), H + min(0, EY[t])
             w_lo, w_hi = max(0, EX[t]), W + min(0, EX[t])
-            nc.vector.tensor_tensor(
-                out=total[:, :, h_lo:h_hi, w_lo:w_hi],
-                in0=total[:, :, h_lo:h_hi, w_lo:w_hi],
-                in1=z[t][:, :, h_lo - EY[t] : h_hi - EY[t], w_lo - EX[t] : w_hi - EX[t]],
-                op=mybir.AluOpType.add,
+            for n in range(IMAGES):
+                nc.vector.tensor_tensor(
+                    out=total[:, n, h_lo:h_hi, w_lo:w_hi],
+                    in0=total[:, n, h_lo:h_hi, w_lo:w_hi],
+                    in1=z[t][:, n, h_lo - EY[t] : h_hi - EY[t], w_lo - EX[t] : w_hi - EX[t]],
+                    op=mybir.AluOpType.add,
+                )
+        for n, queue in enumerate((nc.sync, nc.scalar)):
+            queue.dma_start(
+                out=out[n].rearrange("c h w -> c (h w)"),
+                in_=total[:, n].rearrange("p h w -> p (h w)"),
             )
-        nc.sync.dma_start(
-            out=out.rearrange("n c h w -> c n (h w)"),
-            in_=total[:].rearrange("p n h w -> p n (h w)"),
-        )

@@ -24,7 +24,7 @@ PASSES = CO // K_PASS
 FLOPS = 2 * CO * CI * TAPS * COLUMNS
 BYTES = 2 * CO * CI * TAPS + 2 * IMAGES * CO * PIXELS + 4 * IMAGES * CI * PIXELS
 
-TAPS_FIRST = 4
+QUANTISE_TAPS = ((0, 2), (2, 4), (4, 5))
 
 TAPS_A = slice(0, 3)
 TAPS_B = slice(3, 5)
@@ -48,23 +48,14 @@ def tile_spatialconv_pa_k_kernel(tc, x, weight, grad_out, out):
 
         z = [psum.tile([P, IMAGES, H, W], F32, name="z%d" % t) for t in range(TAPS)]
 
-        grouped = {}
-        quantised = {}
+        g_grouped_of = {}
+        g_quantised_of = {}
+        w_grouped_of = {}
+        w_quantised_of = {}
 
-        def load_and_regroup(g):
+        def load_and_regroup_grad(g):
             g_raw = raw.tile([P, IMAGES, PACK, PIXELS], BF16)
             nc.sync.dma_start(out=g_raw[:].rearrange("p n j x -> p n (j x)"), in_=g_rows[g])
-            w_raw = raw.tile([P, PACK, CI, TAPS], BF16)
-            nc.sync.dma_start(out=w_raw[:].rearrange("p j c t -> p (j c t)"), in_=w_rows[g])
-
-            w_grouped = work.tile([P, TAPS, CI, PACK], BF16, align_bytes=64)
-
-            def regroup_weight(copy, taps, channels):
-                copy(
-                    out=w_grouped[:, taps, channels].rearrange("p t (b i) j -> p b j t i", i=2),
-                    in_=w_raw[:, :, channels, taps].rearrange("p j (b i) t -> p b j t i", i=2),
-                )
-
             g_grouped = work.tile([P, IMAGES, PIXELS, PACK], BF16, align_bytes=64)
 
             def regroup_grad(copy, pixels):
@@ -75,12 +66,25 @@ def tile_spatialconv_pa_k_kernel(tc, x, weight, grad_out, out):
 
             regroup_grad(nc.vector.tensor_copy, slice(PIXELS - VECTOR_PIXELS, PIXELS))
             regroup_grad(nc.scalar.copy, slice(0, PIXELS - VECTOR_PIXELS))
-            regroup_weight(nc.vector.tensor_copy, TAPS_A, slice(0, CI))
-            regroup_weight(nc.scalar.copy, TAPS_B, slice(0, CI))
-            grouped[g] = (w_grouped, g_grouped)
+            g_grouped_of[g] = g_grouped
 
-        def quantise(g):
-            w_grouped, g_grouped = grouped.pop(g)
+        def load_and_regroup_weight(g):
+            w_raw = raw.tile([P, PACK, CI, TAPS], BF16)
+            nc.sync.dma_start(out=w_raw[:].rearrange("p j c t -> p (j c t)"), in_=w_rows[g])
+            w_grouped = work.tile([P, TAPS, CI, PACK], BF16, align_bytes=64)
+
+            def regroup_weight(copy, taps):
+                copy(
+                    out=w_grouped[:, taps].rearrange("p t (b i) j -> p b j t i", i=2),
+                    in_=w_raw[:, :, :, taps].rearrange("p j (b i) t -> p b j t i", i=2),
+                )
+
+            regroup_weight(nc.vector.tensor_copy, TAPS_A)
+            regroup_weight(nc.scalar.copy, TAPS_B)
+            w_grouped_of[g] = w_grouped
+
+        def quantise_grad(g):
+            g_grouped = g_grouped_of.pop(g)
             g_codes = work.tile([P, COLUMNS], U32, align_bytes=64)
             g_scales = work.tile([P, COLUMNS], U8, align_bytes=64)
             nc.vector.quantize_mx(
@@ -88,19 +92,25 @@ def tile_spatialconv_pa_k_kernel(tc, x, weight, grad_out, out):
                 scales=g_scales[:],
                 in_=g_grouped[:].rearrange("p n x j -> p (n x j)"),
             )
+            g_quantised_of[g] = (g_codes, g_scales)
+
+        def quantise_weight(g):
+            w_grouped = w_grouped_of.pop(g)
             w_codes = work.tile([P, TAPS * CI], U32, align_bytes=64)
             w_scales = work.tile([P, TAPS * CI], U8, align_bytes=64)
             w_flat = w_grouped[:].rearrange("p t c j -> p (t c j)")
-            for lo, hi in ((0, TAPS_FIRST * CI), (TAPS_FIRST * CI, TAPS * CI)):
+            for t_lo, t_hi in QUANTISE_TAPS:
+                lo, hi = t_lo * CI, t_hi * CI
                 nc.vector.quantize_mx(
                     out=w_codes[:, lo:hi].bitcast(E4M3X4),
                     scales=w_scales[:, lo:hi],
                     in_=w_flat[:, PACK * lo : PACK * hi],
                 )
-            quantised[g] = (w_codes, w_scales, g_codes, g_scales)
+            w_quantised_of[g] = (w_codes, w_scales)
 
         def multiply(g):
-            w_codes, w_scales, g_codes, g_scales = quantised.pop(g)
+            w_codes, w_scales = w_quantised_of.pop(g)
+            g_codes, g_scales = g_quantised_of.pop(g)
             for t in range(TAPS):
                 nc.tensor.matmul_mx(
                     out=z[t][:].rearrange("p n h w -> p (n h w)"),
@@ -112,9 +122,15 @@ def tile_spatialconv_pa_k_kernel(tc, x, weight, grad_out, out):
                     stop=(g == PASSES - 1),
                 )
 
+        load_and_regroup_grad(0)
+        quantise_grad(0)
         for g in range(PASSES):
-            load_and_regroup(g)
-            quantise(g)
+            if g + 1 < PASSES:
+                load_and_regroup_grad(g + 1)
+            load_and_regroup_weight(g)
+            if g + 1 < PASSES:
+                quantise_grad(g + 1)
+            quantise_weight(g)
             multiply(g)
 
         total = last.tile([P, IMAGES, H, W], F32)

from contextlib import ExitStack

import concourse.mybir as mybir

BF16 = mybir.dt.bfloat16
F32 = mybir.dt.float32
U32 = mybir.dt.uint32
U8 = mybir.dt.uint8
E4M3X4 = mybir.dt.float8_e4m3fn_x4
E5M2X4 = mybir.dt.float8_e5m2_x4

P = 128
PACK = 4
K_PASS = P * PACK

IMAGES, CI, H, W, CO = 2, 128, 16, 16, 16384
PIXELS = H * W
COLUMNS = IMAGES * PIXELS
EY = (0, -1, 0, 0, 1)
EX = (0, 0, -1, 1, 0)
TAPS = len(EY)
PASSES = CO // K_PASS

FLOPS = 2 * CO * CI * TAPS * COLUMNS
BYTES = 2 * CO * CI * TAPS + 2 * IMAGES * CO * PIXELS + 4 * IMAGES * CI * PIXELS

QUANTISE_TAPS = ((0, 2), (2, 4), (4, 5))

TAPS_A = slice(0, 3)
TAPS_B = slice(3, 5)
VECTOR_PIXELS = 96

RAW_BUFS = 6
WORK_BUFS = 3


def tile_spatialconv_pa_k_kernel(tc, x, weight, grad_out, out):
    nc = tc.nc
    w_rows = weight.rearrange("(g p j) c t -> g p (j c t)", p=P, j=PACK)
    g_rows = grad_out.rearrange("n (g p j) h w -> g p n (j h w)", p=P, j=PACK)

    with ExitStack() as ctx:
        raw = ctx.enter_context(tc.tile_pool(name="raw", bufs=RAW_BUFS))
        work = ctx.enter_context(tc.tile_pool(name="work", bufs=WORK_BUFS))
        last = ctx.enter_context(tc.tile_pool(name="last", bufs=1))
        psum = ctx.enter_context(tc.psum_pool(name="psum", bufs=1))
        ctx.enter_context(tc.manual_schedule())

        z = [psum.tile([P, IMAGES, H, W], F32, name="z%d" % t) for t in range(TAPS)]

        g_grouped_of = {}
        g_quantised_of = {}
        w_grouped_of = {}
        w_quantised_of = {}

        def load_and_regroup_grad(g):
            g_raw = raw.tile([P, IMAGES, PACK, PIXELS], BF16)
            nc.sync.dma_start(out=g_raw[:].rearrange("p n j x -> p n (j x)"), in_=g_rows[g])
            g_grouped = work.tile([P, IMAGES, PIXELS, PACK], BF16, align_bytes=64)

            def regroup_grad(copy, pixels):
                copy(
                    out=g_grouped[:, :, pixels].rearrange("p n (b i) j -> p n b j i", i=4),
                    in_=g_raw[:, :, :, pixels].rearrange("p n j (b i) -> p n b j i", i=4),
                )

            regroup_grad(nc.vector.tensor_copy, slice(PIXELS - VECTOR_PIXELS, PIXELS))
            regroup_grad(nc.scalar.copy, slice(0, PIXELS - VECTOR_PIXELS))
            g_grouped_of[g] = g_grouped

        def load_and_regroup_weight(g):
            w_raw = raw.tile([P, PACK, CI, TAPS], BF16)
            nc.sync.dma_start(out=w_raw[:].rearrange("p j c t -> p (j c t)"), in_=w_rows[g])
            w_grouped = work.tile([P, TAPS, CI, PACK], BF16, align_bytes=64)

            def regroup_weight(copy, taps):
                copy(
                    out=w_grouped[:, taps].rearrange("p t (b i) j -> p b j t i", i=2),
                    in_=w_raw[:, :, :, taps].rearrange("p j (b i) t -> p b j t i", i=2),
                )

            regroup_weight(nc.vector.tensor_copy, TAPS_A)
            regroup_weight(nc.scalar.copy, TAPS_B)
            w_grouped_of[g] = w_grouped

        def quantise_grad(g):
            g_grouped = g_grouped_of.pop(g)
            g_codes = work.tile([P, COLUMNS], U32, align_bytes=64)
            g_scales = work.tile([P, COLUMNS], U8, align_bytes=64)
            nc.vector.quantize_mx(
                out=g_codes[:].bitcast(E5M2X4),
                scales=g_scales[:],
                in_=g_grouped[:].rearrange("p n x j -> p (n x j)"),
            )
            g_quantised_of[g] = (g_codes, g_scales)

        def quantise_weight(g):
            w_grouped = w_grouped_of.pop(g)
            w_codes = work.tile([P, TAPS * CI], U32, align_bytes=64)
            w_scales = work.tile([P, TAPS * CI], U8, align_bytes=64)
            w_flat = w_grouped[:].rearrange("p t c j -> p (t c j)")
            for t_lo, t_hi in QUANTISE_TAPS:
                lo, hi = t_lo * CI, t_hi * CI
                nc.vector.quantize_mx(
                    out=w_codes[:, lo:hi].bitcast(E4M3X4),
                    scales=w_scales[:, lo:hi],
                    in_=w_flat[:, PACK * lo : PACK * hi],
                )
            w_quantised_of[g] = (w_codes, w_scales)

        def multiply(g):
            w_codes, w_scales = w_quantised_of.pop(g)
            g_codes, g_scales = g_quantised_of.pop(g)
            for t in range(TAPS):
                nc.tensor.matmul_mx(
                    out=z[t][:].rearrange("p n h w -> p (n h w)"),
                    lhsT=w_codes[:, t * CI : (t + 1) * CI].bitcast(E4M3X4),
                    lhsT_scale=w_scales[:, t * CI : (t + 1) * CI],
                    rhs=g_codes[:].bitcast(E5M2X4),
                    rhs_scale=g_scales[:],
                    start=(g == 0),
                    stop=(g == PASSES - 1),
                )

        load_and_regroup_grad(0)
        quantise_grad(0)
        for g in range(PASSES):
            if g + 1 < PASSES:
                load_and_regroup_grad(g + 1)
            load_and_regroup_weight(g)
            if g + 1 < PASSES:
                quantise_grad(g + 1)
            quantise_weight(g)
            multiply(g)

        total = last.tile([P, IMAGES, H, W], F32)
        for n in range(IMAGES):
            nc.scalar.copy(out=total[:, n], in_=z[0][:, n])
        for t in range(1, TAPS):
            h_lo, h_hi = max(0, EY[t]), H + min(0, EY[t])
            w_lo, w_hi = max(0, EX[t]), W + min(0, EX[t])
            for n in range(IMAGES):
                nc.vector.tensor_tensor(
                    out=total[:, n, h_lo:h_hi, w_lo:w_hi],
                    in0=total[:, n, h_lo:h_hi, w_lo:w_hi],
                    in1=z[t][:, n, h_lo - EY[t] : h_hi - EY[t], w_lo - EX[t] : w_hi - EX[t]],
                    op=mybir.AluOpType.add,
                )
        for n, queue in enumerate((nc.sync, nc.scalar)):
            queue.dma_start(
                out=out[n].rearrange("c h w -> c (h w)"),
                in_=total[:, n].rearrange("p h w -> p (h w)"),
            )
